import numpy as np
import ml_dtypes


def mxq(x, axis, fmt="e4m3"):
    dtype, down = {"e4m3": (ml_dtypes.float8_e4m3fn, 7), "e5m2": (ml_dtypes.float8_e5m2, 14)}[fmt]
    v = np.moveaxis(np.asarray(x, np.float32).astype(ml_dtypes.bfloat16).astype(np.float64), axis, -1)
    blocks = v.reshape(v.shape[:-1] + (-1, 32))
    amax = np.abs(blocks).max(-1, keepdims=True)
    byte = np.maximum(np.where(amax > 0, np.frexp(amax)[1] - 1 + 127, 0) - down, 1)
    scale = np.exp2(byte - 127.0)
    codes = (blocks / scale).astype(np.float32).astype(dtype).astype(np.float64)
    return np.moveaxis((codes * scale).reshape(v.shape), -1, axis)


WIDE = False


def mx_kscale(k):
    if not WIDE:
        return np.ones(k)
    levels = np.array([10, -10, 5, -5, 0])
    a = np.random.permutation(np.resize(levels, k // 512 * 4)).reshape(k // 512, 4)
    idx = np.arange(k)
    return np.exp2(a[idx // 512, idx % 128 // 32])


BF16 = ml_dtypes.bfloat16


def bf(x):
    return np.asarray(x, np.float32).astype(BF16)


def f64(x):
    return np.asarray(x).astype(np.float64)


B, S, C, H, D = 2, 256, 256, 8, 128
E = H * D
EPS = 1e-15


def setup_inputs():
    t = mx_kscale(E)
    return {"q_feat": bf(np.maximum(np.random.standard_normal((B, H, S, D)), 0.0)),
            "vk": bf(np.random.standard_normal((B, H, D, D)) * np.sqrt(S) * t.reshape(H, D)[None, :, :, None]),
            "k_sum": bf(S * (0.11 + 0.02 * np.random.standard_normal((B, H, D)))),
            "Wo": bf(np.random.standard_normal((C, E)) * 6.0 / np.sqrt(E) / t[None, :]),
            "bo": bf(np.random.standard_normal(C) * 0.1)}


def reference(q_feat, vk, k_sum, Wo, bo):
    hs = f64(vk) @ f64(q_feat).transpose(0, 1, 3, 2)
    den = (f64(q_feat) * f64(k_sum)[:, :, None, :]).sum(-1)
    hs = hs / (den[:, :, None, :] + EPS)
    a = hs.transpose(0, 3, 1, 2).reshape(B, S, E)
    return (mxq(a, 2, "e4m3") @ mxq(f64(Wo), 1, "e4m3").T) + f64(bo)

@@ -1,0 +1,155 @@
+import concourse.mybir as mybir
+from concourse.masks import make_identity
+
+F32 = mybir.dt.float32
+BF16 = mybir.dt.bfloat16
+U32 = mybir.dt.uint32
+U8 = mybir.dt.uint8
+FP8X4 = mybir.dt.float8_e4m3fn_x4
+MULT = mybir.AluOpType.mult
+ADD = mybir.AluOpType.add
+
+P = 128
+PACK = 4
+B, H, S, D, C = 2, 8, 256, 128, 256
+EPS = 1e-15
+TOKEN_TILES = S // P
+GROUPS = H // PACK
+UNITS = B * GROUPS
+C_TILES = C // P
+
+FLOPS = 2 * B * H * S * D * D + 2 * B * H * S * D + 2 * B * S * H * D * C
+
+
+def tile_lineartransformerblock_pc_s_kernel(tc, q_feat, vk, k_sum, Wo, bo, out):
+    nc = tc.nc
+    with tc.tile_pool(name="keep", bufs=1) as keep, tc.psum_pool(name="psum", bufs=2) as psum:
+        ks_rows = keep.tile([P, D], BF16)
+        nc.vector.memset(ks_rows[:], 0.0)
+        nc.sync.dma_start(out=ks_rows[0 : B * H, :], in_=k_sum.rearrange("b h d -> (b h) d"))
+
+        vk_sb = [keep.tile([P, PACK, D], BF16, name="vk_sb%d" % u) for u in range(UNITS)]
+        q_sb = [keep.tile([P, PACK, TOKEN_TILES, D], BF16, name="q_sb%d" % u) for u in range(UNITS)]
+        wo_sb = keep.tile([P, C_TILES, H * D], BF16)
+        bias = keep.tile([P, C], BF16)
+
+        def load_unit(u):
+            b, g = divmod(u, GROUPS)
+            heads = slice(PACK * g, PACK * (g + 1))
+            nc.sync.dma_start(out=vk_sb[u][:], in_=vk[b, heads].rearrange("h n d -> n h d"))
+            nc.sync.dma_start(out=q_sb[u][:], in_=q_feat[b, heads].rearrange("h (p j) d -> p h j d", j=TOKEN_TILES))
+
+        load_unit(0)
+        nc.sync.dma_start(out=wo_sb[:], in_=Wo.rearrange("(ct p) k -> p ct k", p=P))
+        for u in range(1, UNITS):
+            load_unit(u)
+        nc.sync.dma_start(out=bias[:], in_=bo.partition_broadcast(P))
+
+        ident = keep.tile([P, P], BF16)
+        make_identity(nc, ident[:])
+
+        ksT_ps = psum.tile([P, PACK, P], BF16, tag="tin")
+        nc.tensor.transpose(ksT_ps[:, 0, :], ks_rows[:], ident[:])
+        ksT = keep.tile([P, B * H], BF16)
+        nc.scalar.copy(out=ksT[:], in_=ksT_ps[:, 0, 0 : B * H])
+
+        vkT = [keep.tile([P, PACK, D], BF16, name="vkT%d" % u) for u in range(UNITS)]
+        qT = [keep.tile([P, TOKEN_TILES, PACK, P], BF16, name="qT%d" % u) for u in range(UNITS)]
+        a_sb = [keep.tile([P, TOKEN_TILES, PACK, D], BF16, name="a_sb%d" % u) for u in range(UNITS)]
+        a_grouped = [keep.tile([P, TOKEN_TILES, P, PACK], BF16, name="a_grouped%d" % u, align_bytes=64) for u in range(UNITS)]
+        a_codes = [keep.tile([P, TOKEN_TILES, P], U32, name="a_codes%d" % u, align_bytes=64) for u in range(UNITS)]
+        a_scales = [keep.tile([P, TOKEN_TILES, P], U8, name="a_scales%d" % u, align_bytes=64) for u in range(UNITS)]
+        w_grouped = keep.tile([P, GROUPS, C, PACK], BF16, align_bytes=64)
+        w_codes = keep.tile([P, GROUPS, C], U32, align_bytes=64)
+        w_scales = keep.tile([P, GROUPS, C], U8, align_bytes=64)
+
+        def transpose_inputs(u):
+            vkT_ps = psum.tile([P, PACK, P], BF16, tag="tin")
+            for t in range(PACK):
+                nc.tensor.transpose(vkT_ps[:, t, :], vk_sb[u][:, t, :], ident[:])
+            nc.scalar.copy(out=vkT[u][:], in_=vkT_ps[:])
+            for j in range(TOKEN_TILES):
+                qT_ps = psum.tile([P, PACK, P], BF16, tag="tin")
+                for t in range(PACK):
+                    nc.tensor.transpose(qT_ps[:, t, :], q_sb[u][:, t, j, :], ident[:])
+                nc.scalar.copy(out=qT[u][:, j, :, :], in_=qT_ps[:])
+
+        def quantise_wo():
+            for g in range(GROUPS):
+                for ct in range(C_TILES):
+                    woT_ps = psum.tile([P, PACK, P], BF16, tag="tin")
+                    for t in range(PACK):
+                        h = PACK * g + t
+                        nc.tensor.transpose(woT_ps[:, t, :], wo_sb[:, ct, D * h : D * (h + 1)], ident[:])
+                    nc.vector.tensor_copy(
+                        out=w_grouped[:, g, P * ct : P * (ct + 1), :], in_=woT_ps[:].rearrange("n t c -> n c t")
+                    )
+            nc.vector.quantize_mx(
+                out=w_codes[:].rearrange("n g c -> n (g c)").bitcast(FP8X4),
+                scales=w_scales[:].rearrange("n g c -> n (g c)"),
+                in_=w_grouped[:].rearrange("n g c t -> n (g c t)"),
+            )
+
+        def read_out(u):
+            den_ps = psum.tile([P, TOKEN_TILES, PACK], F32, tag="den", bufs=1)
+            for j in range(TOKEN_TILES):
+                for t in range(PACK):
+                    bh = PACK * u + t
+                    nc.tensor.matmul(
+                        out=den_ps[:, j, t : t + 1], lhsT=qT[u][:, j, t, :], rhs=ksT[:, bh : bh + 1], start=True, stop=True
+                    )
+            den = keep.tile([P, TOKEN_TILES, PACK], F32, name="den%d" % u)
+            nc.vector.tensor_scalar_add(out=den[:], in0=den_ps[:], scalar1=EPS)
+            recip = keep.tile([P, TOKEN_TILES, PACK], F32, name="recip%d" % u)
+            nc.vector.reciprocal(out=recip[:], in_=den[:])
+            for j in range(TOKEN_TILES):
+                hs_ps = psum.tile([P, PACK, D], F32, tag="hs", bufs=3)
+                for t in range(PACK):
+                    nc.tensor.matmul(out=hs_ps[:, t, :], lhsT=qT[u][:, j, t, :], rhs=vkT[u][:, t, :], start=True, stop=True)
+                nc.vector.tensor_tensor(
+                    out=a_sb[u][:, j, :, :], in0=hs_ps[:], in1=recip[:, j, :].unsqueeze(2).to_broadcast([P, PACK, D]), op=MULT
+                )
+
+        def quantise_a(u):
+            for j in range(TOKEN_TILES):
+                aT_ps = psum.tile([P, PACK, P], BF16, tag="aT")
+                for t in range(PACK):
+                    nc.tensor.transpose(aT_ps[:, t, :], a_sb[u][:, j, t, :], ident[:])
+                nc.scalar.copy(out=a_grouped[u][:, j, :, :], in_=aT_ps[:].rearrange("n t p -> n p t"))
+            nc.vector.quantize_mx(
+                out=a_codes[u][:].rearrange("n j p -> n (j p)").bitcast(FP8X4),
+                scales=a_scales[u][:].rearrange("n j p -> n (j p)"),
+                in_=a_grouped[u][:].rearrange("n j p t -> n (j p t)"),
+            )
+
+        def project(b):
+            out_ps = psum.tile([P, TOKEN_TILES, C], F32, tag="hs", bufs=3)
+            for j in range(TOKEN_TILES):
+                for g in range(GROUPS):
+                    u = GROUPS * b + g
+                    nc.tensor.matmul_mx(
+                        out=out_ps[:, j, :],
+                        lhsT=a_codes[u][:, j, :].bitcast(FP8X4),
+                        lhsT_scale=a_scales[u][:, j, :],
+                        rhs=w_codes[:, g, :].bitcast(FP8X4),
+                        rhs_scale=w_scales[:, g, :],
+                        start=(g == 0),
+                        stop=(g == GROUPS - 1),
+                    )
+            out_sb = keep.tile([P, TOKEN_TILES, C], F32, name="out_sb%d" % b)
+            nc.vector.tensor_tensor(
+                out=out_sb[:], in0=out_ps[:], in1=bias[:].unsqueeze(1).to_broadcast([P, TOKEN_TILES, C]), op=ADD
+            )
+            nc.sync.dma_start(out=out[b].rearrange("(p j) c -> p j c", j=TOKEN_TILES), in_=out_sb[:])
+
+        for step in range(UNITS + 2):
+            if step < UNITS:
+                transpose_inputs(step)
+            if step == 0:
+                quantise_wo()
+            if 1 <= step <= UNITS:
+                read_out(step - 1)
+            if step >= 2:
+                quantise_a(step - 2)
+        for b in range(B):
+            project(b)

@@ -17,6 +17,7 @@ TOKEN_TILES = S // P
 GROUPS = H // PACK
 UNITS = B * GROUPS
 C_TILES = C // P
+HALVES = 2
 
 FLOPS = 2 * B * H * S * D * D + 2 * B * H * S * D + 2 * B * S * H * D * C
 
@@ -47,15 +48,17 @@ def tile_lineartransformerblock_pc_s_kernel(tc, q_feat, vk, k_sum, Wo, bo, out):
 
         ident = keep.tile([P, P], BF16)
         make_identity(nc, ident[:])
+        ident_f32 = keep.tile([P, P], F32)
+        make_identity(nc, ident_f32[:])
 
-        ksT_ps = psum.tile([P, PACK, P], BF16, tag="tin")
+        ksT_ps = psum.tile([P, PACK, P], BF16, tag="tin", bufs=3)
         nc.tensor.transpose(ksT_ps[:, 0, :], ks_rows[:], ident[:])
         ksT = keep.tile([P, B * H], BF16)
         nc.scalar.copy(out=ksT[:], in_=ksT_ps[:, 0, 0 : B * H])
 
         vkT = [keep.tile([P, PACK, D], BF16, name="vkT%d" % u) for u in range(UNITS)]
         qT = [keep.tile([P, TOKEN_TILES, PACK, P], BF16, name="qT%d" % u) for u in range(UNITS)]
-        a_sb = [keep.tile([P, TOKEN_TILES, PACK, D], BF16, name="a_sb%d" % u) for u in range(UNITS)]
+        a_sb = [keep.tile([P, TOKEN_TILES, HALVES, PACK, D // HALVES], BF16, name="a_sb%d" % u) for u in range(UNITS)]
         a_grouped = [keep.tile([P, TOKEN_TILES, P, PACK], BF16, name="a_grouped%d" % u, align_bytes=64) for u in range(UNITS)]
         a_codes = [keep.tile([P, TOKEN_TILES, P], U32, name="a_codes%d" % u, align_bytes=64) for u in range(UNITS)]
         a_scales = [keep.tile([P, TOKEN_TILES, P], U8, name="a_scales%d" % u, align_bytes=64) for u in range(UNITS)]
@@ -64,26 +67,27 @@ def tile_lineartransformerblock_pc_s_kernel(tc, q_feat, vk, k_sum, Wo, bo, out):
         w_scales = keep.tile([P, GROUPS, C], U8, align_bytes=64)
 
         def transpose_inputs(u):
-            vkT_ps = psum.tile([P, PACK, P], BF16, tag="tin")
+            vkT_ps = psum.tile([P, PACK, P], BF16, tag="tin", bufs=3)
             for t in range(PACK):
                 nc.tensor.transpose(vkT_ps[:, t, :], vk_sb[u][:, t, :], ident[:])
             nc.scalar.copy(out=vkT[u][:], in_=vkT_ps[:])
             for j in range(TOKEN_TILES):
-                qT_ps = psum.tile([P, PACK, P], BF16, tag="tin")
+                qT_ps = psum.tile([P, PACK, P], BF16, tag="tin", bufs=3)
                 for t in range(PACK):
                     nc.tensor.transpose(qT_ps[:, t, :], q_sb[u][:, t, j, :], ident[:])
                 nc.scalar.copy(out=qT[u][:, j, :, :], in_=qT_ps[:])
 
         def quantise_wo():
+            wo_words = wo_sb[:].bitcast(F32)
             for g in range(GROUPS):
-                for ct in range(C_TILES):
-                    woT_ps = psum.tile([P, PACK, P], BF16, tag="tin")
-                    for t in range(PACK):
-                        h = PACK * g + t
-                        nc.tensor.transpose(woT_ps[:, t, :], wo_sb[:, ct, D * h : D * (h + 1)], ident[:])
-                    nc.vector.tensor_copy(
-                        out=w_grouped[:, g, P * ct : P * (ct + 1), :], in_=woT_ps[:].rearrange("n t c -> n c t")
-                    )
+                woT_ps = psum.tile([P, HALVES, C], F32, tag="tin", bufs=3)
+                for w in range(HALVES):
+                    first = (HALVES * g + w) * P
+                    for ct in range(C_TILES):
+                        nc.tensor.transpose(
+                            woT_ps[:, w, P * ct : P * (ct + 1)], wo_words[:, ct, first : first + P], ident_f32[:]
+                        )
+                nc.vector.tensor_copy(out=w_grouped[:, g, :, :].bitcast(F32), in_=woT_ps[:].rearrange("p w c -> p c w"))
             nc.vector.quantize_mx(
                 out=w_codes[:].rearrange("n g c -> n (g c)").bitcast(FP8X4),
                 scales=w_scales[:].rearrange("n g c -> n (g c)"),
@@ -103,44 +107,52 @@ def tile_lineartransformerblock_pc_s_kernel(tc, q_feat, vk, k_sum, Wo, bo, out):
             recip = keep.tile([P, TOKEN_TILES, PACK], F32, name="recip%d" % u)
             nc.vector.reciprocal(out=recip[:], in_=den[:])
             for j in range(TOKEN_TILES):
-                hs_ps = psum.tile([P, PACK, D], F32, tag="hs", bufs=3)
+                hs_ps = psum.tile([P, HALVES, PACK, D // HALVES], F32, tag="hs")
                 for t in range(PACK):
-                    nc.tensor.matmul(out=hs_ps[:, t, :], lhsT=qT[u][:, j, t, :], rhs=vkT[u][:, t, :], start=True, stop=True)
+                    nc.tensor.matmul(
+                        out=hs_ps[:, :, t, :],
+                        lhsT=qT[u][:, j, t, :],
+                        rhs=vkT[u][:, t, :].rearrange("d (m e) -> d e m", e=HALVES),
+                        start=True,
+                        stop=True,
+                    )
                 nc.vector.tensor_tensor(
-                    out=a_sb[u][:, j, :, :], in0=hs_ps[:], in1=recip[:, j, :].unsqueeze(2).to_broadcast([P, PACK, D]), op=MULT
+                    out=a_sb[u][:, j, :, :, :],
+                    in0=hs_ps[:],
+                    in1=recip[:, j, :].unsqueeze(1).unsqueeze(3).to_broadcast([P, HALVES, PACK, D // HALVES]),
+                    op=MULT,
                 )
 
         def quantise_a(u):
             for j in range(TOKEN_TILES):
                 aT_ps = psum.tile([P, PACK, P], BF16, tag="aT")
-                for t in range(PACK):
-                    nc.tensor.transpose(aT_ps[:, t, :], a_sb[u][:, j, t, :], ident[:])
+                for w in range(HALVES):
+                    for e in range(HALVES):
+                        two_heads = a_sb[u][:, j, e, HALVES * w : HALVES * (w + 1), :].rearrange("p h m -> p (h m)")
+                        nc.tensor.transpose(aT_ps[:, HALVES * w + e, :], two_heads, ident[:])
                 nc.scalar.copy(out=a_grouped[u][:, j, :, :], in_=aT_ps[:].rearrange("n t p -> n p t"))
-            nc.vector.quantize_mx(
-                out=a_codes[u][:].rearrange("n j p -> n (j p)").bitcast(FP8X4),
-                scales=a_scales[u][:].rearrange("n j p -> n (j p)"),
-                in_=a_grouped[u][:].rearrange("n j p t -> n (j p t)"),
-            )
+                nc.vector.quantize_mx(
+                    out=a_codes[u][:, j, :].bitcast(FP8X4),
+                    scales=a_scales[u][:, j, :],
+                    in_=a_grouped[u][:, j, :, :].rearrange("n p t -> n (p t)"),
+                )
 
-        def project(b):
-            out_ps = psum.tile([P, TOKEN_TILES, C], F32, tag="hs", bufs=3)
-            for j in range(TOKEN_TILES):
-                for g in range(GROUPS):
-                    u = GROUPS * b + g
-                    nc.tensor.matmul_mx(
-                        out=out_ps[:, j, :],
-                        lhsT=a_codes[u][:, j, :].bitcast(FP8X4),
-                        lhsT_scale=a_scales[u][:, j, :],
-                        rhs=w_codes[:, g, :].bitcast(FP8X4),
-                        rhs_scale=w_scales[:, g, :],
-                        start=(g == 0),
-                        stop=(g == GROUPS - 1),
-                    )
-            out_sb = keep.tile([P, TOKEN_TILES, C], F32, name="out_sb%d" % b)
-            nc.vector.tensor_tensor(
-                out=out_sb[:], in0=out_ps[:], in1=bias[:].unsqueeze(1).to_broadcast([P, TOKEN_TILES, C]), op=ADD
-            )
-            nc.sync.dma_start(out=out[b].rearrange("(p j) c -> p j c", j=TOKEN_TILES), in_=out_sb[:])
+        def project(b, j):
+            out_ps = psum.tile([P, C], F32, tag="hs")
+            for g in range(GROUPS):
+                u = GROUPS * b + g
+                nc.tensor.matmul_mx(
+                    out=out_ps[:],
+                    lhsT=a_codes[u][:, j, :].bitcast(FP8X4),
+                    lhsT_scale=a_scales[u][:, j, :],
+                    rhs=w_codes[:, g, :].bitcast(FP8X4),
+                    rhs_scale=w_scales[:, g, :],
+                    start=(g == 0),
+                    stop=(g == GROUPS - 1),
+                )
+            out_sb = keep.tile([P, C], F32, name="out_sb%d%d" % (b, j))
+            nc.vector.tensor_tensor(out=out_sb[:], in0=out_ps[:], in1=bias[:], op=ADD)
+            nc.sync.dma_start(out=out[b].rearrange("(p j) c -> p j c", j=TOKEN_TILES)[:, j, :], in_=out_sb[:])
 
         for step in range(UNITS + 2):
             if step < UNITS:
@@ -152,4 +164,5 @@ def tile_lineartransformerblock_pc_s_kernel(tc, q_feat, vk, k_sum, Wo, bo, out):
             if step >= 2:
                 quantise_a(step - 2)
         for b in range(B):
-            project(b)
+            for j in range(TOKEN_TILES):
+                project(b, j)

@@ -5,6 +5,7 @@ F32 = mybir.dt.float32
 BF16 = mybir.dt.bfloat16
 U32 = mybir.dt.uint32
 U8 = mybir.dt.uint8
+I32 = mybir.dt.int32
 FP8X4 = mybir.dt.float8_e4m3fn_x4
 MULT = mybir.AluOpType.mult
 ADD = mybir.AluOpType.add
@@ -17,6 +18,8 @@ TOKEN_TILES = S // P
 GROUPS = H // PACK
 UNITS = B * GROUPS
 C_TILES = C // P
+WARM_PASSES = 8
+WARM_COLUMNS = 256
 HALVES = 2
 
 FLOPS = 2 * B * H * S * D * D + 2 * B * H * S * D + 2 * B * S * H * D * C
@@ -45,6 +48,23 @@ def tile_lineartransformerblock_pc_s_kernel(tc, q_feat, vk, k_sum, Wo, bo, out):
         for u in range(1, UNITS):
             load_unit(u)
         nc.sync.dma_start(out=bias[:], in_=bo.partition_broadcast(P))
+
+        warm_codes = keep.tile([P, WARM_COLUMNS], U32, align_bytes=64)
+        warm_scales = keep.tile([P, WARM_COLUMNS], U8, align_bytes=64)
+        zeros = keep.tile([P, PACK * WARM_COLUMNS], BF16, align_bytes=64)
+        nc.vector.memset(zeros[:].bitcast(I32), 0)
+        nc.vector.quantize_mx(out=warm_codes[:].bitcast(FP8X4), scales=warm_scales[:], in_=zeros[:])
+        warm_ps = psum.tile([P, WARM_COLUMNS], F32, tag="hs")
+        for i in range(WARM_PASSES):
+            nc.tensor.matmul_mx(
+                out=warm_ps[:],
+                lhsT=warm_codes[:, 0:P].bitcast(FP8X4),
+                lhsT_scale=warm_scales[:, 0:P],
+                rhs=warm_codes[:].bitcast(FP8X4),
+                rhs_scale=warm_scales[:],
+                start=True,
+                stop=True,
+            )
 
         ident = keep.tile([P, P], BF16)
         make_identity(nc, ident[:])

@@ -5,7 +5,6 @@ F32 = mybir.dt.float32
 BF16 = mybir.dt.bfloat16
 U32 = mybir.dt.uint32
 U8 = mybir.dt.uint8
-I32 = mybir.dt.int32
 FP8X4 = mybir.dt.float8_e4m3fn_x4
 MULT = mybir.AluOpType.mult
 ADD = mybir.AluOpType.add
@@ -18,8 +17,6 @@ TOKEN_TILES = S // P
 GROUPS = H // PACK
 UNITS = B * GROUPS
 C_TILES = C // P
-WARM_PASSES = 8
-WARM_COLUMNS = 256
 HALVES = 2
 
 FLOPS = 2 * B * H * S * D * D + 2 * B * H * S * D + 2 * B * S * H * D * C
@@ -44,27 +41,11 @@ def tile_lineartransformerblock_pc_s_kernel(tc, q_feat, vk, k_sum, Wo, bo, out):
             nc.sync.dma_start(out=q_sb[u][:], in_=q_feat[b, heads].rearrange("h (p j) d -> p h j d", j=TOKEN_TILES))
 
         load_unit(0)
+        load_unit(1)
         nc.sync.dma_start(out=wo_sb[:], in_=Wo.rearrange("(ct p) k -> p ct k", p=P))
-        for u in range(1, UNITS):
+        for u in range(2, UNITS):
             load_unit(u)
         nc.sync.dma_start(out=bias[:], in_=bo.partition_broadcast(P))
-
-        warm_codes = keep.tile([P, WARM_COLUMNS], U32, align_bytes=64)
-        warm_scales = keep.tile([P, WARM_COLUMNS], U8, align_bytes=64)
-        zeros = keep.tile([P, PACK * WARM_COLUMNS], BF16, align_bytes=64)
-        nc.vector.memset(zeros[:].bitcast(I32), 0)
-        nc.vector.quantize_mx(out=warm_codes[:].bitcast(FP8X4), scales=warm_scales[:], in_=zeros[:])
-        warm_ps = psum.tile([P, WARM_COLUMNS], F32, tag="hs")
-        for i in range(WARM_PASSES):
-            nc.tensor.matmul_mx(
-                out=warm_ps[:],
-                lhsT=warm_codes[:, 0:P].bitcast(FP8X4),
-                lhsT_scale=warm_scales[:, 0:P],
-                rhs=warm_codes[:].bitcast(FP8X4),
-                rhs_scale=warm_scales[:],
-                start=True,
-                stop=True,
-            )
 
         ident = keep.tile([P, P], BF16)
         make_identity(nc, ident[:])
@@ -114,7 +95,9 @@ def tile_lineartransformerblock_pc_s_kernel(tc, q_feat, vk, k_sum, Wo, bo, out):
                 in_=w_grouped[:].rearrange("n g c t -> n (g c t)"),
             )
 
-        def read_out(u):
+        recip = [keep.tile([P, TOKEN_TILES, PACK], F32, name="recip%d" % u) for u in range(UNITS)]
+
+        def denominators(u):
             den_ps = psum.tile([P, TOKEN_TILES, PACK], F32, tag="den", bufs=1)
             for j in range(TOKEN_TILES):
                 for t in range(PACK):
@@ -124,8 +107,9 @@ def tile_lineartransformerblock_pc_s_kernel(tc, q_feat, vk, k_sum, Wo, bo, out):
                     )
             den = keep.tile([P, TOKEN_TILES, PACK], F32, name="den%d" % u)
             nc.vector.tensor_scalar_add(out=den[:], in0=den_ps[:], scalar1=EPS)
-            recip = keep.tile([P, TOKEN_TILES, PACK], F32, name="recip%d" % u)
-            nc.vector.reciprocal(out=recip[:], in_=den[:])
+            nc.vector.reciprocal(out=recip[u][:], in_=den[:])
+
+        def read_out(u):
             for j in range(TOKEN_TILES):
                 hs_ps = psum.tile([P, HALVES, PACK, D // HALVES], F32, tag="hs")
                 for t in range(PACK):
@@ -139,7 +123,7 @@ def tile_lineartransformerblock_pc_s_kernel(tc, q_feat, vk, k_sum, Wo, bo, out):
                 nc.vector.tensor_tensor(
                     out=a_sb[u][:, j, :, :, :],
                     in0=hs_ps[:],
-                    in1=recip[:, j, :].unsqueeze(1).unsqueeze(3).to_broadcast([P, HALVES, PACK, D // HALVES]),
+                    in1=recip[u][:, j, :].unsqueeze(1).unsqueeze(3).to_broadcast([P, HALVES, PACK, D // HALVES]),
                     op=MULT,
                 )
 
@@ -177,10 +161,11 @@ def tile_lineartransformerblock_pc_s_kernel(tc, q_feat, vk, k_sum, Wo, bo, out):
         for step in range(UNITS + 2):
             if step < UNITS:
                 transpose_inputs(step)
-            if step == 0:
-                quantise_wo()
+                denominators(step)
             if 1 <= step <= UNITS:
                 read_out(step - 1)
+            if step == 1:
+                quantise_wo()
             if step >= 2:
                 quantise_a(step - 2)
         for b in range(B):

@@ -18,6 +18,8 @@ GROUPS = H // PACK
 UNITS = B * GROUPS
 C_TILES = C // P
 HALVES = 2
+VK_ROWS = PACK * D // P
+VK_RUN = D // VK_ROWS
 
 FLOPS = 2 * B * H * S * D * D + 2 * B * H * S * D + 2 * B * S * H * D * C
 
@@ -29,7 +31,7 @@ def tile_lineartransformerblock_pc_s_kernel(tc, q_feat, vk, k_sum, Wo, bo, out):
         nc.vector.memset(ks_rows[:], 0.0)
         nc.sync.dma_start(out=ks_rows[0 : B * H, :], in_=k_sum.rearrange("b h d -> (b h) d"))
 
-        vk_sb = [keep.tile([P, PACK, D], BF16, name="vk_sb%d" % u) for u in range(UNITS)]
+        vk_sb = [keep.tile([P, VK_ROWS, D], BF16, name="vk_sb%d" % u) for u in range(UNITS)]
         q_sb = [keep.tile([P, PACK, TOKEN_TILES, D], BF16, name="q_sb%d" % u) for u in range(UNITS)]
         wo_sb = keep.tile([P, C_TILES, H * D], BF16)
         bias = keep.tile([P, C], BF16)
@@ -37,7 +39,7 @@ def tile_lineartransformerblock_pc_s_kernel(tc, q_feat, vk, k_sum, Wo, bo, out):
         def load_unit(u):
             b, g = divmod(u, GROUPS)
             heads = slice(PACK * g, PACK * (g + 1))
-            nc.sync.dma_start(out=vk_sb[u][:], in_=vk[b, heads].rearrange("h n d -> n h d"))
+            nc.sync.dma_start(out=vk_sb[u][:], in_=vk[b, heads].rearrange("h (r i) d -> (h r) i d", i=VK_ROWS))
             nc.sync.dma_start(out=q_sb[u][:], in_=q_feat[b, heads].rearrange("h (p j) d -> p h j d", j=TOKEN_TILES))
 
         load_unit(0)
@@ -57,7 +59,7 @@ def tile_lineartransformerblock_pc_s_kernel(tc, q_feat, vk, k_sum, Wo, bo, out):
         ksT = keep.tile([P, B * H], BF16)
         nc.scalar.copy(out=ksT[:], in_=ksT_ps[:, 0, 0 : B * H])
 
-        vkT = [keep.tile([P, PACK, D], BF16, name="vkT%d" % u) for u in range(UNITS)]
+        vkT = [keep.tile([P, VK_ROWS, P], BF16, name="vkT%d" % u) for u in range(UNITS)]
         qT = [keep.tile([P, TOKEN_TILES, PACK, P], BF16, name="qT%d" % u) for u in range(UNITS)]
         a_sb = [keep.tile([P, TOKEN_TILES, HALVES, PACK, D // HALVES], BF16, name="a_sb%d" % u) for u in range(UNITS)]
         a_grouped = [keep.tile([P, TOKEN_TILES, P, PACK], BF16, name="a_grouped%d" % u, align_bytes=64) for u in range(UNITS)]
@@ -68,9 +70,9 @@ def tile_lineartransformerblock_pc_s_kernel(tc, q_feat, vk, k_sum, Wo, bo, out):
         w_scales = keep.tile([P, GROUPS, C], U8, align_bytes=64)
 
         def transpose_inputs(u):
-            vkT_ps = psum.tile([P, PACK, P], BF16, tag="tin", bufs=3)
-            for t in range(PACK):
-                nc.tensor.transpose(vkT_ps[:, t, :], vk_sb[u][:, t, :], ident[:])
+            vkT_ps = psum.tile([P, VK_ROWS, P], BF16, tag="tin", bufs=3)
+            for i in range(VK_ROWS):
+                nc.tensor.transpose(vkT_ps[:, i, :], vk_sb[u][:, i, :], ident[:])
             nc.scalar.copy(out=vkT[u][:], in_=vkT_ps[:])
             for j in range(TOKEN_TILES):
                 qT_ps = psum.tile([P, PACK, P], BF16, tag="tin", bufs=3)
@@ -114,9 +116,9 @@ def tile_lineartransformerblock_pc_s_kernel(tc, q_feat, vk, k_sum, Wo, bo, out):
                 hs_ps = psum.tile([P, HALVES, PACK, D // HALVES], F32, tag="hs")
                 for t in range(PACK):
                     nc.tensor.matmul(
-                        out=hs_ps[:, :, t, :],
+                        out=hs_ps[:, :, t, :].rearrange("p e (r i2) -> p i2 e r", i2=HALVES),
                         lhsT=qT[u][:, j, t, :],
-                        rhs=vkT[u][:, t, :].rearrange("d (m e) -> d e m", e=HALVES),
+                        rhs=vkT[u][:, :, VK_RUN * t : VK_RUN * (t + 1)].rearrange("d (i2 e) r -> d i2 e r", e=HALVES),
                         start=True,
                         stop=True,
                     )

@@ -18,8 +18,6 @@ GROUPS = H // PACK
 UNITS = B * GROUPS
 C_TILES = C // P
 HALVES = 2
-VK_ROWS = PACK * D // P
-VK_RUN = D // VK_ROWS
 
 FLOPS = 2 * B * H * S * D * D + 2 * B * H * S * D + 2 * B * S * H * D * C
 
@@ -30,16 +28,20 @@ def tile_lineartransformerblock_pc_s_kernel(tc, q_feat, vk, k_sum, Wo, bo, out):
         ks_rows = keep.tile([P, D], BF16)
         nc.vector.memset(ks_rows[:], 0.0)
         nc.sync.dma_start(out=ks_rows[0 : B * H, :], in_=k_sum.rearrange("b h d -> (b h) d"))
+        bo_rows = keep.tile([P, C], BF16)
+        nc.vector.memset(bo_rows[:], 0.0)
+        nc.sync.dma_start(out=bo_rows[0:1, :], in_=bo.unsqueeze(0))
+        ones = keep.tile([P, P], BF16)
+        nc.vector.memset(ones[:], 1.0)
 
-        vk_sb = [keep.tile([P, VK_ROWS, D], BF16, name="vk_sb%d" % u) for u in range(UNITS)]
+        vk_sb = [keep.tile([P, PACK, D], BF16, name="vk_sb%d" % u) for u in range(UNITS)]
         q_sb = [keep.tile([P, PACK, TOKEN_TILES, D], BF16, name="q_sb%d" % u) for u in range(UNITS)]
         wo_sb = keep.tile([P, C_TILES, H * D], BF16)
-        bias = keep.tile([P, C], BF16)
 
         def load_unit(u):
             b, g = divmod(u, GROUPS)
             heads = slice(PACK * g, PACK * (g + 1))
-            nc.sync.dma_start(out=vk_sb[u][:], in_=vk[b, heads].rearrange("h (r i) d -> (h r) i d", i=VK_ROWS))
+            nc.sync.dma_start(out=vk_sb[u][:], in_=vk[b, heads].rearrange("h n d -> n h d"))
             nc.sync.dma_start(out=q_sb[u][:], in_=q_feat[b, heads].rearrange("h (p j) d -> p h j d", j=TOKEN_TILES))
 
         load_unit(0)
@@ -47,7 +49,6 @@ def tile_lineartransformerblock_pc_s_kernel(tc, q_feat, vk, k_sum, Wo, bo, out):
         nc.sync.dma_start(out=wo_sb[:], in_=Wo.rearrange("(ct p) k -> p ct k", p=P))
         for u in range(2, UNITS):
             load_unit(u)
-        nc.sync.dma_start(out=bias[:], in_=bo.partition_broadcast(P))
 
         ident = keep.tile([P, P], BF16)
         make_identity(nc, ident[:])
@@ -59,7 +60,12 @@ def tile_lineartransformerblock_pc_s_kernel(tc, q_feat, vk, k_sum, Wo, bo, out):
         ksT = keep.tile([P, B * H], BF16)
         nc.scalar.copy(out=ksT[:], in_=ksT_ps[:, 0, 0 : B * H])
 
-        vkT = [keep.tile([P, VK_ROWS, P], BF16, name="vkT%d" % u) for u in range(UNITS)]
+        bias_ps = psum.tile([P, C], F32, tag="tin", bufs=3)
+        nc.tensor.matmul(out=bias_ps[:], lhsT=ones[:], rhs=bo_rows[:], start=True, stop=True)
+        bias = keep.tile([P, C], F32)
+        nc.scalar.copy(out=bias[:], in_=bias_ps[:])
+
+        vkT = [keep.tile([P, PACK, D], BF16, name="vkT%d" % u) for u in range(UNITS)]
         qT = [keep.tile([P, TOKEN_TILES, PACK, P], BF16, name="qT%d" % u) for u in range(UNITS)]
         a_sb = [keep.tile([P, TOKEN_TILES, HALVES, PACK, D // HALVES], BF16, name="a_sb%d" % u) for u in range(UNITS)]
         a_grouped = [keep.tile([P, TOKEN_TILES, P, PACK], BF16, name="a_grouped%d" % u, align_bytes=64) for u in range(UNITS)]
@@ -70,9 +76,9 @@ def tile_lineartransformerblock_pc_s_kernel(tc, q_feat, vk, k_sum, Wo, bo, out):
         w_scales = keep.tile([P, GROUPS, C], U8, align_bytes=64)
 
         def transpose_inputs(u):
-            vkT_ps = psum.tile([P, VK_ROWS, P], BF16, tag="tin", bufs=3)
-            for i in range(VK_ROWS):
-                nc.tensor.transpose(vkT_ps[:, i, :], vk_sb[u][:, i, :], ident[:])
+            vkT_ps = psum.tile([P, PACK, P], BF16, tag="tin", bufs=3)
+            for t in range(PACK):
+                nc.tensor.transpose(vkT_ps[:, t, :], vk_sb[u][:, t, :], ident[:])
             nc.scalar.copy(out=vkT[u][:], in_=vkT_ps[:])
             for j in range(TOKEN_TILES):
                 qT_ps = psum.tile([P, PACK, P], BF16, tag="tin", bufs=3)
@@ -97,6 +103,7 @@ def tile_lineartransformerblock_pc_s_kernel(tc, q_feat, vk, k_sum, Wo, bo, out):
                 in_=w_grouped[:].rearrange("n g c t -> n (g c t)"),
             )
 
+        den = [keep.tile([P, TOKEN_TILES, PACK], F32, name="den%d" % u) for u in range(UNITS)]
         recip = [keep.tile([P, TOKEN_TILES, PACK], F32, name="recip%d" % u) for u in range(UNITS)]
 
         def denominators(u):
@@ -107,18 +114,19 @@ def tile_lineartransformerblock_pc_s_kernel(tc, q_feat, vk, k_sum, Wo, bo, out):
                     nc.tensor.matmul(
                         out=den_ps[:, j, t : t + 1], lhsT=qT[u][:, j, t, :], rhs=ksT[:, bh : bh + 1], start=True, stop=True
                     )
-            den = keep.tile([P, TOKEN_TILES, PACK], F32, name="den%d" % u)
-            nc.vector.tensor_scalar_add(out=den[:], in0=den_ps[:], scalar1=EPS)
-            nc.vector.reciprocal(out=recip[u][:], in_=den[:])
+            nc.vector.tensor_scalar_add(out=den[u][:], in0=den_ps[:], scalar1=EPS)
+
+        def reciprocals(u):
+            nc.vector.reciprocal(out=recip[u][:], in_=den[u][:])
 
         def read_out(u):
             for j in range(TOKEN_TILES):
                 hs_ps = psum.tile([P, HALVES, PACK, D // HALVES], F32, tag="hs")
                 for t in range(PACK):
                     nc.tensor.matmul(
-                        out=hs_ps[:, :, t, :].rearrange("p e (r i2) -> p i2 e r", i2=HALVES),
+                        out=hs_ps[:, :, t, :],
                         lhsT=qT[u][:, j, t, :],
-                        rhs=vkT[u][:, :, VK_RUN * t : VK_RUN * (t + 1)].rearrange("d (i2 e) r -> d i2 e r", e=HALVES),
+                        rhs=vkT[u][:, t, :].rearrange("d (m e) -> d e m", e=HALVES),
                         start=True,
                         stop=True,
                     )
@@ -166,6 +174,8 @@ def tile_lineartransformerblock_pc_s_kernel(tc, q_feat, vk, k_sum, Wo, bo, out):
                 denominators(step)
             if 1 <= step <= UNITS:
                 read_out(step - 1)
+            if step < UNITS:
+                reciprocals(step)
             if step == 1:
                 quantise_wo()
             if step >= 2:

import concourse.mybir as mybir
from concourse.masks import make_identity

F32 = mybir.dt.float32
BF16 = mybir.dt.bfloat16
U32 = mybir.dt.uint32
U8 = mybir.dt.uint8
FP8X4 = mybir.dt.float8_e4m3fn_x4
MULT = mybir.AluOpType.mult
ADD = mybir.AluOpType.add

P = 128
PACK = 4
B, H, S, D, C = 2, 8, 256, 128, 256
EPS = 1e-15
TOKEN_TILES = S // P
GROUPS = H // PACK
UNITS = B * GROUPS
C_TILES = C // P
HALVES = 2

FLOPS = 2 * B * H * S * D * D + 2 * B * H * S * D + 2 * B * S * H * D * C


def tile_lineartransformerblock_pc_s_kernel(tc, q_feat, vk, k_sum, Wo, bo, out):
    nc = tc.nc
    with tc.tile_pool(name="keep", bufs=1) as keep, tc.psum_pool(name="psum", bufs=2) as psum:
        ks_rows = keep.tile([P, D], BF16)
        nc.vector.memset(ks_rows[:], 0.0)
        nc.sync.dma_start(out=ks_rows[0 : B * H, :], in_=k_sum.rearrange("b h d -> (b h) d"))
        bo_rows = keep.tile([P, C], BF16)
        nc.vector.memset(bo_rows[:], 0.0)
        nc.sync.dma_start(out=bo_rows[0:1, :], in_=bo.unsqueeze(0))
        ones = keep.tile([P, P], BF16)
        nc.vector.memset(ones[:], 1.0)

        vk_sb = [keep.tile([P, PACK, D], BF16, name="vk_sb%d" % u) for u in range(UNITS)]
        q_sb = [keep.tile([P, PACK, TOKEN_TILES, D], BF16, name="q_sb%d" % u) for u in range(UNITS)]
        wo_sb = keep.tile([P, C_TILES, H * D], BF16)

        def load_unit(u):
            b, g = divmod(u, GROUPS)
            heads = slice(PACK * g, PACK * (g + 1))
            nc.sync.dma_start(out=vk_sb[u][:], in_=vk[b, heads].rearrange("h n d -> n h d"))
            nc.sync.dma_start(out=q_sb[u][:], in_=q_feat[b, heads].rearrange("h (p j) d -> p h j d", j=TOKEN_TILES))

        load_unit(0)
        load_unit(1)
        nc.sync.dma_start(out=wo_sb[:], in_=Wo.rearrange("(ct p) k -> p ct k", p=P))
        for u in range(2, UNITS):
            load_unit(u)

        ident = keep.tile([P, P], BF16)
        make_identity(nc, ident[:])
        ident_f32 = keep.tile([P, P], F32)
        make_identity(nc, ident_f32[:])

        ksT_ps = psum.tile([P, PACK, P], BF16, tag="tin", bufs=3)
        nc.tensor.transpose(ksT_ps[:, 0, :], ks_rows[:], ident[:])
        ksT = keep.tile([P, B * H], BF16)
        nc.scalar.copy(out=ksT[:], in_=ksT_ps[:, 0, 0 : B * H])

        bias_ps = psum.tile([P, C], F32, tag="tin", bufs=3)
        nc.tensor.matmul(out=bias_ps[:], lhsT=ones[:], rhs=bo_rows[:], start=True, stop=True)
        bias = keep.tile([P, C], F32)
        nc.scalar.copy(out=bias[:], in_=bias_ps[:])

        vkT = [keep.tile([P, PACK, D], BF16, name="vkT%d" % u) for u in range(UNITS)]
        qT = [keep.tile([P, TOKEN_TILES, PACK, P], BF16, name="qT%d" % u) for u in range(UNITS)]
        a_sb = [keep.tile([P, TOKEN_TILES, HALVES, PACK, D // HALVES], BF16, name="a_sb%d" % u) for u in range(UNITS)]
        a_grouped = [keep.tile([P, TOKEN_TILES, P, PACK], BF16, name="a_grouped%d" % u, align_bytes=64) for u in range(UNITS)]
        a_codes = [keep.tile([P, TOKEN_TILES, P], U32, name="a_codes%d" % u, align_bytes=64) for u in range(UNITS)]
        a_scales = [keep.tile([P, TOKEN_TILES, P], U8, name="a_scales%d" % u, align_bytes=64) for u in range(UNITS)]
        w_grouped = keep.tile([P, GROUPS, C, PACK], BF16, align_bytes=64)
        w_codes = keep.tile([P, GROUPS, C], U32, align_bytes=64)
        w_scales = keep.tile([P, GROUPS, C], U8, align_bytes=64)

        def transpose_inputs(u):
            vkT_ps = psum.tile([P, PACK, P], BF16, tag="tin", bufs=3)
            for t in range(PACK):
                nc.tensor.transpose(vkT_ps[:, t, :], vk_sb[u][:, t, :], ident[:])
            nc.scalar.copy(out=vkT[u][:], in_=vkT_ps[:])
            for j in range(TOKEN_TILES):
                qT_ps = psum.tile([P, PACK, P], BF16, tag="tin", bufs=3)
                for t in range(PACK):
                    nc.tensor.transpose(qT_ps[:, t, :], q_sb[u][:, t, j, :], ident[:])
                nc.scalar.copy(out=qT[u][:, j, :, :], in_=qT_ps[:])

        def quantise_wo():
            wo_words = wo_sb[:].bitcast(F32)
            for g in range(GROUPS):
                woT_ps = psum.tile([P, HALVES, C], F32, tag="tin", bufs=3)
                for w in range(HALVES):
                    first = (HALVES * g + w) * P
                    for ct in range(C_TILES):
                        nc.tensor.transpose(
                            woT_ps[:, w, P * ct : P * (ct + 1)], wo_words[:, ct, first : first + P], ident_f32[:]
                        )
                nc.vector.tensor_copy(out=w_grouped[:, g, :, :].bitcast(F32), in_=woT_ps[:].rearrange("p w c -> p c w"))
            nc.vector.quantize_mx(
                out=w_codes[:].rearrange("n g c -> n (g c)").bitcast(FP8X4),
                scales=w_scales[:].rearrange("n g c -> n (g c)"),
                in_=w_grouped[:].rearrange("n g c t -> n (g c t)"),
            )

        den = [keep.tile([P, TOKEN_TILES, PACK], F32, name="den%d" % u) for u in range(UNITS)]
        recip = [keep.tile([P, TOKEN_TILES, PACK], F32, name="recip%d" % u) for u in range(UNITS)]

        def denominators(u):
            den_ps = psum.tile([P, TOKEN_TILES, PACK], F32, tag="den", bufs=1)
            for j in range(TOKEN_TILES):
                for t in range(PACK):
                    bh = PACK * u + t
                    nc.tensor.matmul(
                        out=den_ps[:, j, t : t + 1], lhsT=qT[u][:, j, t, :], rhs=ksT[:, bh : bh + 1], start=True, stop=True
                    )
            nc.vector.tensor_scalar_add(out=den[u][:], in0=den_ps[:], scalar1=EPS)

        def reciprocals(u):
            nc.vector.reciprocal(out=recip[u][:], in_=den[u][:])

        def read_out(u):
            for j in range(TOKEN_TILES):
                hs_ps = psum.tile([P, HALVES, PACK, D // HALVES], F32, tag="hs")
                for t in range(PACK):
                    nc.tensor.matmul(
                        out=hs_ps[:, :, t, :],
                        lhsT=qT[u][:, j, t, :],
                        rhs=vkT[u][:, t, :].rearrange("d (m e) -> d e m", e=HALVES),
                        start=True,
                        stop=True,
                    )
                nc.vector.tensor_tensor(
                    out=a_sb[u][:, j, :, :, :],
                    in0=hs_ps[:],
                    in1=recip[u][:, j, :].unsqueeze(1).unsqueeze(3).to_broadcast([P, HALVES, PACK, D // HALVES]),
                    op=MULT,
                )

        def quantise_a(u):
            for j in range(TOKEN_TILES):
                aT_ps = psum.tile([P, PACK, P], BF16, tag="aT")
                for w in range(HALVES):
                    for e in range(HALVES):
                        two_heads = a_sb[u][:, j, e, HALVES * w : HALVES * (w + 1), :].rearrange("p h m -> p (h m)")
                        nc.tensor.transpose(aT_ps[:, HALVES * w + e, :], two_heads, ident[:])
                nc.scalar.copy(out=a_grouped[u][:, j, :, :], in_=aT_ps[:].rearrange("n t p -> n p t"))
                nc.vector.quantize_mx(
                    out=a_codes[u][:, j, :].bitcast(FP8X4),
                    scales=a_scales[u][:, j, :],
                    in_=a_grouped[u][:, j, :, :].rearrange("n p t -> n (p t)"),
                )

        def project(b, j):
            out_ps = psum.tile([P, C], F32, tag="hs")
            for g in range(GROUPS):
                u = GROUPS * b + g
                nc.tensor.matmul_mx(
                    out=out_ps[:],
                    lhsT=a_codes[u][:, j, :].bitcast(FP8X4),
                    lhsT_scale=a_scales[u][:, j, :],
                    rhs=w_codes[:, g, :].bitcast(FP8X4),
                    rhs_scale=w_scales[:, g, :],
                    start=(g == 0),
                    stop=(g == GROUPS - 1),
                )
            out_sb = keep.tile([P, C], F32, name="out_sb%d%d" % (b, j))
            nc.vector.tensor_tensor(out=out_sb[:], in0=out_ps[:], in1=bias[:], op=ADD)
            nc.sync.dma_start(out=out[b].rearrange("(p j) c -> p j c", j=TOKEN_TILES)[:, j, :], in_=out_sb[:])

        for step in range(UNITS + 2):
            if step < UNITS:
                transpose_inputs(step)
                denominators(step)
            if 1 <= step <= UNITS:
                read_out(step - 1)
            if step < UNITS:
                reciprocals(step)
            if step == 1:
                quantise_wo()
            if step >= 2:
                quantise_a(step - 2)
        for b in range(B):
            for j in range(TOKEN_TILES):
                project(b, j)
